import numpy as np
import ml_dtypes


def mxq(x, axis, fmt="e4m3"):
    dtype, down = {"e4m3": (ml_dtypes.float8_e4m3fn, 7), "e5m2": (ml_dtypes.float8_e5m2, 14)}[fmt]
    v = np.moveaxis(np.asarray(x, np.float32).astype(ml_dtypes.bfloat16).astype(np.float64), axis, -1)
    blocks = v.reshape(v.shape[:-1] + (-1, 32))
    amax = np.abs(blocks).max(-1, keepdims=True)
    byte = np.maximum(np.where(amax > 0, np.frexp(amax)[1] - 1 + 127, 0) - down, 1)
    scale = np.exp2(byte - 127.0)
    codes = (blocks / scale).astype(np.float32).astype(dtype).astype(np.float64)
    return np.moveaxis((codes * scale).reshape(v.shape), -1, axis)


WIDE = False


def mx_kscale(k):
    if not WIDE:
        return np.ones(k)
    levels = np.array([10, -10, 5, -5, 0])
    if k % 512:
        return np.exp2(np.random.permutation(np.resize(levels, k // 32))).repeat(32)
    a = np.empty((k // 512, 16))
    for p in range(k // 512):
        a[p, :8] = np.random.permutation(np.resize(levels, 8))
        for g in range(8):
            far = levels[np.abs(levels - a[p, g]) >= 10]
            a[p, g + 8] = far[np.random.randint(len(far))]
    return np.exp2(a.ravel()).repeat(32)


BF16 = ml_dtypes.bfloat16


def bf(x):
    return np.asarray(x, np.float32).astype(BF16)


def f64(x):
    return np.asarray(x).astype(np.float64)


B, S, D, H, KV, DH = 4, 512, 1024, 8, 2, 128
T = B * S
QD = H * DH
KD = KV * DH
N = QD + 2 * KD
ROPE_THETA = 10000.0


def apply_rope(x, positions):
    inv_freq = ROPE_THETA ** (-np.arange(0, DH, 2) / DH)
    ang = positions[:, None] * inv_freq[None, :]
    cos = np.cos(ang)[:, None, :]
    sin = np.sin(ang)[:, None, :]
    x1, x2 = x[..., : DH // 2], x[..., DH // 2 :]
    return np.concatenate([x1 * cos - x2 * sin, x2 * cos + x1 * sin], axis=-1)


def draw0():
    s = mx_kscale(D)
    return {"hidden_states": bf(np.random.standard_normal((T, D)) * s),
            "wqkv": bf(np.random.standard_normal((N, D)) / np.sqrt(D) / s[None, :]),
            "bqkv": bf(np.random.standard_normal(N) * 0.3)}


def core(hidden_states, wqkv, bqkv):
    qkv = (mxq(f64(hidden_states), 1, "e4m3") @ mxq(f64(wqkv), 1, "e4m3").T) + f64(bqkv)
    q = qkv[:, :QD].reshape(T, H, DH)
    k = qkv[:, QD : QD + KD].reshape(T, KV, DH)
    v = qkv[:, QD + KD :].reshape(T, KV, DH)
    positions = np.tile(np.arange(S), B)
    q = apply_rope(q, positions)
    k = apply_rope(k, positions)
    return q.reshape(B, S, H, DH), k.reshape(B, S, KV, DH), v.reshape(B, S, KV, DH)


def e4m3fn_bytes(y):
    return np.clip(np.asarray(y, np.float64), -448.0, 448.0).astype(np.float32).astype(ml_dtypes.float8_e4m3fn).view(np.uint8)


def e4m3fn_values(b):
    return np.asarray(b, np.uint8).view(ml_dtypes.float8_e4m3fn).astype(np.float64)


def setup_inputs():
    d = draw0()
    x0 = np.asarray(d['hidden_states']).astype(np.float64)
    s = (np.max(np.abs(x0), axis=(0,), keepdims=True) / 448.0).astype(np.float32)
    out = {}
    for k, v in d.items():
        if k == 'hidden_states':
            out['hidden_states_bytes'] = e4m3fn_bytes(x0 / s.astype(np.float64))
            out['hidden_states_scale'] = s
        else:
            out[k] = v
    return out


def reference(hidden_states_bytes, hidden_states_scale, wqkv, bqkv):
    return core(e4m3fn_values(hidden_states_bytes) * hidden_states_scale.astype(np.float64), wqkv, bqkv)

@@ -1,0 +1,390 @@
+from contextlib import ExitStack
+import math
+
+import concourse.mybir as mybir
+from concourse.masks import make_identity
+
+F32 = mybir.dt.float32
+BF16 = mybir.dt.bfloat16
+I32 = mybir.dt.int32
+U8 = mybir.dt.uint8
+U32 = mybir.dt.uint32
+FP8 = mybir.dt.float8_e4m3fn
+FP8X4 = mybir.dt.float8_e4m3fn_x4
+ALU = mybir.AluOpType
+ACT = mybir.ActivationFunctionType
+
+P = 128
+NB = 4
+S = 512
+D = 1024
+NCT = 12
+NROPE = 10
+STEP_LIST = [(0, 2), (0, 0), (0, 1)] + [(b, cg) for b in range(1, NB) for cg in range(3)]
+STEPS = len(STEP_LIST)
+BANKS = 4
+FLOPS = 2 * 2048 * 1024 * 1536
+TWO_PI = 2.0 * math.pi
+
+
+def tile_flashqwen2attention_pa_kernel(
+    tc, hidden_states_bytes, hidden_states_scale, wqkv, bqkv, out_0, out_1, out_2
+):
+    nc = tc.nc
+    q_out = out_0.rearrange("b s h d -> (b s) (h d)")
+    k_out = out_1.rearrange("b s h d -> (b s) (h d)")
+    v_out = out_2.rearrange("b s h d -> (b s) (h d)")
+    x_rows = hidden_states_bytes.rearrange("(b j p) k -> b p j k", j=4, p=P)
+
+    with ExitStack() as ctx:
+        keep = ctx.enter_context(tc.tile_pool(name="keep", bufs=1))
+        work = ctx.enter_context(tc.tile_pool(name="work", bufs=2))
+        psum = ctx.enter_context(tc.psum_pool(name="psum", bufs=1))
+        ctx.enter_context(tc.manual_schedule())
+
+        brow = keep.tile([P, P], BF16, name="brow")
+        nc.vector.memset(brow[:], 0.0)
+        sc = keep.tile([P, D], F32, name="sc")
+        nc.scalar.dma_start(
+            out=sc[:], in_=hidden_states_scale.rearrange("o k -> (o k)").partition_broadcast(P)
+        )
+        nc.scalar.dma_start(out=brow[0:NCT, :], in_=bqkv.rearrange("(t p) -> t p", p=P))
+        bvraw = keep.tile([P, 2 * P], BF16, name="bvraw")
+        nc.scalar.dma_start(out=bvraw[:], in_=bqkv[NROPE * P:NCT * P].partition_broadcast(P))
+
+        xbytes = []
+        for b in range(NB):
+            xbytes_b = keep.tile([P, 4, D], U8, name="xbytes%d" % b)
+            xbytes.append(xbytes_b)
+        wraw = []
+        for ct in range(NCT):
+            wraw_ct = keep.tile([P, D], BF16, name="wraw%d" % ct)
+            wraw.append(wraw_ct)
+
+        def load_x(b):
+            nc.sync.dma_start(out=xbytes[b][:], in_=x_rows[b])
+
+        def load_w(ct):
+            nc.sync.dma_start(out=wraw[ct][:], in_=wqkv[ct * P:(ct + 1) * P, :])
+
+        for j in range(4):
+            nc.sync.dma_start(out=xbytes[0][:, j, :], in_=x_rows[0][:, j, :])
+            load_w(8 + j)
+        for ct in range(0, 4):
+            load_w(ct)
+        load_x(1)
+        for ct in range(4, 8):
+            load_w(ct)
+        load_x(2)
+        load_x(3)
+
+        warm = keep.tile([P, 1], F32, name="warm")
+        nc.vector.memset(warm[:], 0.0)
+        warm2 = keep.tile([P, 1], F32, name="warm2")
+        nc.scalar.activation(out=warm2[:], in_=warm[:], func=ACT.Sin)
+
+        chan = keep.tile([P, 7], I32, name="chan")
+        nc.gpsimd.iota(chan[:], pattern=[[0, 7]], base=0, channel_multiplier=1)
+        shift = keep.tile([P, 7], I32, name="shift")
+        nc.gpsimd.iota(shift[:], pattern=[[1, 7]], base=0, channel_multiplier=0)
+        pos = keep.tile([P, S], I32, name="pos")
+        nc.gpsimd.iota(pos[:], pattern=[[1, S]], base=0, channel_multiplier=0)
+        ident = keep.tile([P, P], F32, name="ident")
+        make_identity(nc, ident[:])
+        perm = keep.tile([P, P], F32, name="perm")
+        nc.gpsimd.memset(perm[:], 0.0)
+        for base in (64, -64):
+            nc.gpsimd.affine_select(
+                out=perm[:], in_=perm[:], compare_op=ALU.not_equal, fill=1.0,
+                base=base, pattern=[[-1, P]], channel_multiplier=1,
+            )
+
+        bits_i = keep.tile([P, 7], I32, name="bits_i")
+        nc.vector.tensor_tensor(out=bits_i[:], in0=chan[:], in1=shift[:], op=ALU.logical_shift_right)
+        bits_j = keep.tile([P, 7], I32, name="bits_j")
+        nc.vector.tensor_scalar(out=bits_j[:], in0=bits_i[:], scalar1=1, scalar2=None, op0=ALU.bitwise_and)
+        bits = keep.tile([P, 7], F32, name="bits")
+        nc.vector.tensor_copy(out=bits[:], in_=bits_j[:])
+        fac = keep.tile([P, 6], F32, name="fac")
+        for bit in range(6):
+            ratio = 10000.0 ** (-(2.0 ** bit) / 64.0)
+            lead = 1.0 / TWO_PI if bit == 0 else 1.0
+            nc.vector.tensor_scalar(
+                out=fac[:, bit:bit + 1], in0=bits[:, bit:bit + 1],
+                scalar1=(ratio - 1.0) * lead, scalar2=lead, op0=ALU.mult, op1=ALU.add,
+            )
+        fac3 = keep.tile([P, 3], F32, name="fac3")
+        nc.vector.tensor_tensor(out=fac3[:], in0=fac[:, 0:3], in1=fac[:, 3:6], op=ALU.mult)
+        fac1 = keep.tile([P, 1], F32, name="fac1")
+        nc.vector.tensor_tensor(out=fac1[:], in0=fac3[:, 0:1], in1=fac3[:, 1:2], op=ALU.mult)
+        freq = keep.tile([P, 1], F32, name="freq")
+        nc.vector.tensor_tensor(out=freq[:], in0=fac1[:], in1=fac3[:, 2:3], op=ALU.mult)
+        sin_scale = keep.tile([P, 1], F32, name="sin_scale")
+        nc.vector.tensor_scalar(
+            out=sin_scale[:], in0=bits[:, 6:7], scalar1=2.0 * TWO_PI, scalar2=-TWO_PI,
+            op0=ALU.mult, op1=ALU.add,
+        )
+
+        turns = keep.tile([P, S], F32, name="turns")
+        nc.vector.tensor_scalar(out=turns[:], in0=pos[:], scalar1=freq[:, 0:1], scalar2=None, op0=ALU.mult)
+        whole = keep.tile([P, S], I32, name="whole")
+        nc.vector.tensor_scalar(out=whole[:], in0=pos[:], scalar1=freq[:, 0:1], scalar2=None, op0=ALU.mult)
+        frac = keep.tile([P, S], F32, name="frac")
+        nc.vector.tensor_tensor(out=frac[:], in0=turns[:], in1=whole[:], op=ALU.subtract)
+        negfrac = keep.tile([P, S], F32, name="negfrac")
+        nc.vector.scalar_tensor_tensor(
+            out=negfrac[:], in0=frac[:], scalar=0.5, in1=frac[:], op0=ALU.is_gt, op1=ALU.subtract
+        )
+        absfrac = keep.tile([P, S], F32, name="absfrac")
+        nc.scalar.activation(out=absfrac[:], in_=negfrac[:], func=ACT.Abs)
+        table = keep.tile([P, 2, S], F32, name="table")
+        nc.scalar.activation(out=table[:, 0, :], in_=absfrac[:], func=ACT.Sin, bias=0.5 * math.pi, scale=-TWO_PI)
+        nc.scalar.activation(out=table[:, 1, :], in_=negfrac[:], func=ACT.Sin, scale=sin_scale[:, 0:1])
+
+        xcodes = keep.tile([P, NB, 2, S], U32, name="xcodes", align_bytes=64)
+        xscales = keep.tile([P, NB, 2, S], U8, name="xscales", align_bytes=64)
+        wcodes = keep.tile([P, NCT, 2, P], U32, name="wcodes", align_bytes=64)
+        wscales = keep.tile([P, NCT, 2, P], U8, name="wscales", align_bytes=64)
+
+        wvcodes = keep.tile([P, 2, 2 * P], U32, name="wvcodes", align_bytes=64)
+        wvscales = keep.tile([P, 2, 2 * P], U8, name="wvscales", align_bytes=64)
+
+        turned = {}
+
+        def every_second_word(rows_bf16):
+            words = rows_bf16.bitcast(F32)
+            return [[words[:, 256 * g + u:256 * (g + 1):2] for u in range(2)] for g in range(2)]
+
+        def turn(key, quarters, tag):
+            bank = psum.tile([P, 2, 2, P], F32, tag=tag, name=tag, bufs=BANKS)
+            turned[key] = bank
+            for g in range(2):
+                for u in range(2):
+                    nc.tensor.transpose(out=bank[:, g, u, :], in_=quarters[g][u], identity=ident[:])
+
+        def unload(key, dst_words):
+            nc.scalar.copy(out=dst_words, in_=turned[key][:].rearrange("p g u r -> p g r u"))
+
+        wg = {}
+
+        def w_turn(ct, tag):
+            turn(("w", ct), every_second_word(wraw[ct][:]), tag)
+
+        def w_unload(ct):
+            wg_ct = work.tile([P, 2, P, 4], BF16, tag="wg", name="wg", bufs=4, align_bytes=64)
+            wg[ct] = wg_ct
+            unload(("w", ct), wg_ct[:].bitcast(F32))
+
+        def w_quant(ct):
+            if ct >= NROPE:
+                cols = slice((ct - NROPE) * P, (ct - NROPE + 1) * P)
+                for g in range(2):
+                    nc.vector.quantize_mx(
+                        out=wvcodes[:, g, cols].bitcast(FP8X4), scales=wvscales[:, g, cols],
+                        in_=wg[ct][:, g].rearrange("p m t -> p (m t)"),
+                    )
+                return
+            nc.vector.quantize_mx(
+                out=wcodes[:, ct].rearrange("p g m -> p (g m)").bitcast(FP8X4),
+                scales=wscales[:, ct].rearrange("p g m -> p (g m)"),
+                in_=wg[ct][:].rearrange("p g m t -> p (g m t)"),
+            )
+
+        xw = {}
+        xg = {}
+
+        def x_widen(b, j):
+            xw_t = work.tile([P, D], BF16, tag="xw", name="xw", bufs=4)
+            xw[(b, j)] = xw_t
+            nc.vector.tensor_tensor(out=xw_t[:], in0=xbytes[b][:, j, :].bitcast(FP8), in1=sc[:], op=ALU.mult)
+
+        xp = {}
+
+        def x_order(b, j):
+            xp_t = work.tile([P, 2, 2, P], F32, tag="xp", name="xp", bufs=3)
+            xp[(b, j)] = xp_t
+            nc.scalar.copy(out=xp_t[:], in_=xw[(b, j)][:].bitcast(F32).rearrange("p (g w u) -> p g u w", g=2, u=2))
+
+        def x_turn(b, j, tag):
+            if b == 0:
+                quarters = every_second_word(xw[(b, j)][:])
+            else:
+                quarters = [[xp[(b, j)][:, g, u, :] for u in range(2)] for g in range(2)]
+            turn(("x", b, j), quarters, tag)
+
+        def x_unload(b, j):
+            if j == 0:
+                xg_b = work.tile([P, 2, S, 4], BF16, tag="xg", name="xg", bufs=2, align_bytes=64)
+                xg[b] = xg_b
+            unload(("x", b, j), xg[b][:].bitcast(F32)[:, :, j * P:(j + 1) * P, :])
+
+        def x_quant(b, j):
+            for g in range(2):
+                nc.vector.quantize_mx(
+                    out=xcodes[:, b, g, j * P:(j + 1) * P].bitcast(FP8X4),
+                    scales=xscales[:, b, g, j * P:(j + 1) * P],
+                    in_=xg[b][:, g, j * P:(j + 1) * P, :].rearrange("p r t -> p (r t)"),
+                )
+
+        accs = {}
+        tus = {}
+
+        def mx(out, lhs, lhs_s, rhs, rhs_s, g):
+            nc.tensor.matmul_mx(out=out, lhsT=lhs.bitcast(FP8X4), lhsT_scale=lhs_s,
+                                rhs=rhs.bitcast(FP8X4), rhs_scale=rhs_s, start=(g == 0), stop=(g == 1))
+
+        def rope_units(cg):
+            return range(4) if cg < 2 else range(2)
+
+        def multiply(n):
+            b, cg = STEP_LIST[n]
+            for c4 in rope_units(cg):
+                ct = 4 * cg + c4
+                acc = psum.tile([P, S], F32, tag="acc", name="acc", bufs=BANKS)
+                accs[(n, c4)] = acc
+                for g in range(2):
+                    mx(acc[:], wcodes[:, ct, g, :], wscales[:, ct, g, :], xcodes[:, b, g, :], xscales[:, b, g, :], g)
+            if cg == 2:
+                for jp in range(2):
+                    accv = psum.tile([P, 2, 2 * P], F32, tag="acc", name="accv", bufs=BANKS)
+                    accs[(n, 2 + jp)] = accv
+                    for jj in range(2):
+                        toks = slice((2 * jp + jj) * P, (2 * jp + jj + 1) * P)
+                        for g in range(2):
+                            mx(accv[:, jj, :], xcodes[:, b, g, toks], xscales[:, b, g, toks],
+                               wvcodes[:, g, :], wvscales[:, g, :], g)
+
+        def pool_units(n):
+            b, cg = STEP_LIST[n]
+            return (0, 1) if (b == 0 and cg < 2) else (0,)
+
+        def rotate(n):
+            b, cg = STEP_LIST[n]
+            on_pool = pool_units(n)
+            for c4 in rope_units(cg):
+                ct = 4 * cg + c4
+                acc = accs[(n, c4)]
+                tu = work.tile([P, 2, S], F32, tag="tu", name="tu", bufs=8)
+                tus[(n, c4)] = tu
+                if c4 in on_pool:
+                    xs = work.tile([P, S], F32, tag="xs", name="xs", bufs=3)
+                    nc.scalar.activation(
+                        out=xs[:], in_=acc[:], func=ACT.Identity, bias=bcol[:, ct:ct + 1], scale=1.0
+                    )
+                    nc.gpsimd.tensor_tensor(
+                        out=tu[:], in0=xs[:].unsqueeze(1).to_broadcast([P, 2, S]), in1=table[:], op=ALU.mult
+                    )
+                else:
+                    nc.vector.scalar_tensor_tensor(
+                        out=tu[:], in0=acc[:].unsqueeze(1).to_broadcast([P, 2, S]),
+                        scalar=bcol[:, ct:ct + 1], in1=table[:], op0=ALU.add, op1=ALU.mult,
+                    )
+            if cg == 2:
+                for jp in range(2):
+                    vs = work.tile([P, 2, 2 * P], F32, tag="vs", name="vs", bufs=3)
+                    nc.vector.tensor_tensor(
+                        out=vs[:], in0=accs[(n, 2 + jp)][:],
+                        in1=bv[:].unsqueeze(1).to_broadcast([P, 2, 2 * P]), op=ALU.add,
+                    )
+                    r0 = b * S + jp * 2 * P
+                    nc.sync.dma_start(out=v_out[r0:r0 + 2 * P, :].rearrange("(j p) c -> p j c", p=P), in_=vs[:])
+
+        def turn_back(out, tu, toks):
+            nc.tensor.matmul(out=out, lhsT=tu[:, 0, toks], rhs=ident[:], is_transpose=True, start=True, stop=False)
+            nc.tensor.matmul(out=out, lhsT=tu[:, 1, toks], rhs=perm[:], is_transpose=True, start=False, stop=True)
+
+        def blocks_of(n):
+            return 4 if STEP_LIST[n][1] < 2 else 2
+
+        def finish_block(n, blk):
+            b, cg = STEP_LIST[n]
+            ys = work.tile([P, S], F32, tag="ys", name="ys", bufs=8)
+            if cg < 2:
+                ob = psum.tile([P, S], F32, tag="ob", name="ob", bufs=BANKS)
+                toks = slice(blk * P, (blk + 1) * P)
+                for c4 in range(4):
+                    turn_back(ob[:, c4 * P:(c4 + 1) * P], tus[(n, c4)], toks)
+                nc.scalar.copy(out=ys[:], in_=ob[:])
+                r0 = b * S + blk * P
+                nc.sync.dma_start(out=q_out[r0:r0 + P, cg * S:(cg + 1) * S], in_=ys[:])
+            else:
+                obk = psum.tile([P, 2, 2 * P], F32, tag="ob", name="obk", bufs=BANKS)
+                for jj in range(2):
+                    toks = slice((2 * blk + jj) * P, (2 * blk + jj + 1) * P)
+                    for c4 in range(2):
+                        turn_back(obk[:, jj, c4 * P:(c4 + 1) * P], tus[(n, c4)], toks)
+                nc.scalar.copy(out=ys[:], in_=obk[:].rearrange("p j c -> p (j c)"))
+                r0 = b * S + blk * 2 * P
+                nc.sync.dma_start(
+                    out=k_out[r0:r0 + 2 * P, :].rearrange("(j p) c -> p j c", p=P),
+                    in_=ys[:].rearrange("p (j c) -> p j c", j=2),
+                )
+
+        bcol = keep.tile([P, NCT], F32, name="bcol")
+        bv = keep.tile([P, 2 * P], F32, name="bv")
+        brow32 = keep.tile([P, P], F32, name="brow32")
+        x_widen(0, 0)
+        x_widen(0, 1)
+        w_turn(8, "acc")
+        w_unload(8)
+        w_turn(9, "acc")
+        x_turn(0, 0, "ob")
+        x_unload(0, 0)
+        w_unload(9)
+        nc.vector.tensor_copy(out=brow32[:], in_=brow[:])
+        x_widen(0, 2)
+        x_widen(0, 3)
+        x_turn(0, 1, "ob")
+        x_unload(0, 1)
+        bt = psum.tile([P, P], F32, tag="ob", name="bt", bufs=BANKS)
+        nc.tensor.transpose(out=bt[:], in_=brow32[:], identity=ident[:])
+        w_turn(10, "acc")
+        x_turn(0, 2, "ob")
+        x_unload(0, 2)
+        w_turn(11, "acc")
+        x_turn(0, 3, "ob")
+        x_unload(0, 3)
+        w_quant(8)
+        x_quant(0, 0)
+        w_quant(9)
+        x_quant(0, 1)
+        nc.vector.tensor_copy(out=bcol[:], in_=bt[:, 0:NCT])
+        nc.vector.tensor_copy(out=bv[:], in_=bvraw[:])
+        x_quant(0, 2)
+        x_quant(0, 3)
+        w_unload(10)
+        w_unload(11)
+        w_quant(10)
+        w_quant(11)
+
+        for n in range(STEPS):
+            b, cg = STEP_LIST[n]
+            nxt = []
+            if b + 1 < NB:
+                nxt = [(0,), (1,), (2, 3)][n % 3]
+            for j in nxt:
+                x_widen(b + 1, j)
+            multiply(n)
+            rotate(n)
+            for j in nxt:
+                x_order(b + 1, j)
+            jobs = [("x", j) for j in nxt]
+            if n < 2:
+                cg_next = STEP_LIST[n + 1][1]
+                jobs = [("w", ct) for ct in range(4 * cg_next, 4 * cg_next + 4)] + jobs
+            nblk = blocks_of(n - 1) if n > 0 else 0
+            for i in range(max(nblk, len(jobs))):
+                if i < len(jobs):
+                    kind, idx = jobs[i]
+                    if kind == "w":
+                        w_turn(idx, "ob")
+                        w_unload(idx)
+                        w_quant(idx)
+                    else:
+                        x_turn(b + 1, idx, "ob")
+                        x_unload(b + 1, idx)
+                        x_quant(b + 1, idx)
+                if i < nblk:
+                    finish_block(n - 1, i)
+        for blk in range(blocks_of(STEPS - 1)):
+            finish_block(STEPS - 1, blk)

@@ -218,12 +218,13 @@ def tile_flashqwen2attention_pa_kernel(
                 xg[b] = xg_b
             unload(("x", b, j), xg[b][:].bitcast(F32)[:, :, j * P:(j + 1) * P, :])
 
-        def x_quant(b, j):
+        def x_quant(b, j0):
+            toks = slice(j0 * P, (j0 + 2) * P)
             for g in range(2):
                 nc.vector.quantize_mx(
-                    out=xcodes[:, b, g, j * P:(j + 1) * P].bitcast(FP8X4),
-                    scales=xscales[:, b, g, j * P:(j + 1) * P],
-                    in_=xg[b][:, g, j * P:(j + 1) * P, :].rearrange("p r t -> p (r t)"),
+                    out=xcodes[:, b, g, toks].bitcast(FP8X4),
+                    scales=xscales[:, b, g, toks],
+                    in_=xg[b][:, g, toks, :].rearrange("p r t -> p (r t)"),
                 )
 
         accs = {}
@@ -345,13 +346,11 @@ def tile_flashqwen2attention_pa_kernel(
         x_turn(0, 3, "ob")
         x_unload(0, 3)
         w_quant(8)
-        x_quant(0, 0)
         w_quant(9)
-        x_quant(0, 1)
+        x_quant(0, 0)
         nc.vector.tensor_copy(out=bcol[:], in_=bt[:, 0:NCT])
         nc.vector.tensor_copy(out=bv[:], in_=bvraw[:])
         x_quant(0, 2)
-        x_quant(0, 3)
         w_unload(10)
         w_unload(11)
         w_quant(10)
@@ -383,7 +382,8 @@ def tile_flashqwen2attention_pa_kernel(
                     else:
                         x_turn(b + 1, idx, "ob")
                         x_unload(b + 1, idx)
-                        x_quant(b + 1, idx)
+                        if idx % 2 == 1:
+                            x_quant(b + 1, idx - 1)
                 if i < nblk:
                     finish_block(n - 1, i)
         for blk in range(blocks_of(STEPS - 1)):

@@ -43,7 +43,7 @@ def tile_flashqwen2attention_pa_kernel(
         ctx.enter_context(tc.manual_schedule())
 
         brow = keep.tile([P, P], BF16, name="brow")
-        nc.vector.memset(brow[:], 0.0)
+        nc.gpsimd.memset(brow[:], 0.0)
         sc = keep.tile([P, D], F32, name="sc")
         nc.scalar.dma_start(
             out=sc[:], in_=hidden_states_scale.rearrange("o k -> (o k)").partition_broadcast(P)
@@ -79,7 +79,7 @@ def tile_flashqwen2attention_pa_kernel(
         load_x(3)
 
         warm = keep.tile([P, 1], F32, name="warm")
-        nc.vector.memset(warm[:], 0.0)
+        nc.gpsimd.memset(warm[:], 0.0)
         warm2 = keep.tile([P, 1], F32, name="warm2")
         nc.scalar.activation(out=warm2[:], in_=warm[:], func=ACT.Sin)
 
@@ -98,6 +98,9 @@ def tile_flashqwen2attention_pa_kernel(
                 out=perm[:], in_=perm[:], compare_op=ALU.not_equal, fill=1.0,
                 base=base, pattern=[[-1, P]], channel_multiplier=1,
             )
+
+        ident_bf = keep.tile([P, P], BF16, name="ident_bf")
+        make_identity(nc, ident_bf[:])
 
         bits_i = keep.tile([P, 7], I32, name="bits_i")
         nc.vector.tensor_tensor(out=bits_i[:], in0=chan[:], in1=shift[:], op=ALU.logical_shift_right)
@@ -125,12 +128,12 @@ def tile_flashqwen2attention_pa_kernel(
             op0=ALU.mult, op1=ALU.add,
         )
 
-        turns = keep.tile([P, S], F32, name="turns")
-        nc.vector.tensor_scalar(out=turns[:], in0=pos[:], scalar1=freq[:, 0:1], scalar2=None, op0=ALU.mult)
         whole = keep.tile([P, S], I32, name="whole")
         nc.vector.tensor_scalar(out=whole[:], in0=pos[:], scalar1=freq[:, 0:1], scalar2=None, op0=ALU.mult)
         frac = keep.tile([P, S], F32, name="frac")
-        nc.vector.tensor_tensor(out=frac[:], in0=turns[:], in1=whole[:], op=ALU.subtract)
+        nc.vector.scalar_tensor_tensor(
+            out=frac[:], in0=pos[:], scalar=freq[:, 0:1], in1=whole[:], op0=ALU.mult, op1=ALU.subtract
+        )
         negfrac = keep.tile([P, S], F32, name="negfrac")
         nc.vector.scalar_tensor_tensor(
             out=negfrac[:], in0=frac[:], scalar=0.5, in1=frac[:], op0=ALU.is_gt, op1=ALU.subtract
@@ -141,8 +144,8 @@ def tile_flashqwen2attention_pa_kernel(
         nc.scalar.activation(out=table[:, 0, :], in_=absfrac[:], func=ACT.Sin, bias=0.5 * math.pi, scale=-TWO_PI)
         nc.scalar.activation(out=table[:, 1, :], in_=negfrac[:], func=ACT.Sin, scale=sin_scale[:, 0:1])
 
-        xcodes = keep.tile([P, NB, 2, S], U32, name="xcodes", align_bytes=64)
-        xscales = keep.tile([P, NB, 2, S], U8, name="xscales", align_bytes=64)
+        xcodes = keep.tile([P, NB, 2, 2, S // 2], U32, name="xcodes", align_bytes=64)
+        xscales = keep.tile([P, NB, 2, 2, S // 2], U8, name="xscales", align_bytes=64)
         wcodes = keep.tile([P, NCT, 2, P], U32, name="wcodes", align_bytes=64)
         wscales = keep.tile([P, NCT, 2, P], U8, name="wscales", align_bytes=64)
 
@@ -170,19 +173,24 @@ def tile_flashqwen2attention_pa_kernel(
         def w_turn(ct, tag):
             turn(("w", ct), every_second_word(wraw[ct][:]), tag)
 
+        wgv = keep.tile([P, 2, 2 * P, 4], BF16, name="wgv", align_bytes=64)
+
         def w_unload(ct):
+            if ct >= NROPE:
+                cols = slice((ct - NROPE) * P, (ct - NROPE + 1) * P)
+                unload(("w", ct), wgv[:].bitcast(F32)[:, :, cols, :])
+                return
             wg_ct = work.tile([P, 2, P, 4], BF16, tag="wg", name="wg", bufs=4, align_bytes=64)
             wg[ct] = wg_ct
             unload(("w", ct), wg_ct[:].bitcast(F32))
 
         def w_quant(ct):
             if ct >= NROPE:
-                cols = slice((ct - NROPE) * P, (ct - NROPE + 1) * P)
-                for g in range(2):
-                    nc.vector.quantize_mx(
-                        out=wvcodes[:, g, cols].bitcast(FP8X4), scales=wvscales[:, g, cols],
-                        in_=wg[ct][:, g].rearrange("p m t -> p (m t)"),
-                    )
+                nc.vector.quantize_mx(
+                    out=wvcodes[:].rearrange("p g c -> p (g c)").bitcast(FP8X4),
+                    scales=wvscales[:].rearrange("p g c -> p (g c)"),
+                    in_=wgv[:].rearrange("p g c t -> p (g c t)"),
+                )
                 return
             nc.vector.quantize_mx(
                 out=wcodes[:, ct].rearrange("p g m -> p (g m)").bitcast(FP8X4),
@@ -206,7 +214,7 @@ def tile_flashqwen2attention_pa_kernel(
             nc.scalar.copy(out=xp_t[:], in_=xw[(b, j)][:].bitcast(F32).rearrange("p (g w u) -> p g u w", g=2, u=2))
 
         def x_turn(b, j, tag):
-            if b == 0:
+            if b <= 1:
                 quarters = every_second_word(xw[(b, j)][:])
             else:
                 quarters = [[xp[(b, j)][:, g, u, :] for u in range(2)] for g in range(2)]
@@ -214,18 +222,17 @@ def tile_flashqwen2attention_pa_kernel(
 
         def x_unload(b, j):
             if j == 0:
-                xg_b = work.tile([P, 2, S, 4], BF16, tag="xg", name="xg", bufs=2, align_bytes=64)
+                xg_b = work.tile([P, 2, 2, S // 2, 4], BF16, tag="xg", name="xg", bufs=2, align_bytes=64)
                 xg[b] = xg_b
-            unload(("x", b, j), xg[b][:].bitcast(F32)[:, :, j * P:(j + 1) * P, :])
+            unload(("x", b, j), xg[b][:, j // 2].bitcast(F32)[:, :, (j % 2) * P:(j % 2 + 1) * P, :])
 
         def x_quant(b, j0):
-            toks = slice(j0 * P, (j0 + 2) * P)
-            for g in range(2):
-                nc.vector.quantize_mx(
-                    out=xcodes[:, b, g, toks].bitcast(FP8X4),
-                    scales=xscales[:, b, g, toks],
-                    in_=xg[b][:, g, toks, :].rearrange("p r t -> p (r t)"),
-                )
+            h = j0 // 2
+            nc.vector.quantize_mx(
+                out=xcodes[:, b, h].rearrange("p g r -> p (g r)").bitcast(FP8X4),
+                scales=xscales[:, b, h].rearrange("p g r -> p (g r)"),
+                in_=xg[b][:, h].rearrange("p g r t -> p (g r t)"),
+            )
 
         accs = {}
         tus = {}
@@ -243,16 +250,18 @@ def tile_flashqwen2attention_pa_kernel(
                 ct = 4 * cg + c4
                 acc = psum.tile([P, S], F32, tag="acc", name="acc", bufs=BANKS)
                 accs[(n, c4)] = acc
-                for g in range(2):
-                    mx(acc[:], wcodes[:, ct, g, :], wscales[:, ct, g, :], xcodes[:, b, g, :], xscales[:, b, g, :], g)
+                for h in range(2):
+                    for g in range(2):
+                        mx(acc[:, h * (S // 2):(h + 1) * (S // 2)], wcodes[:, ct, g, :], wscales[:, ct, g, :],
+                           xcodes[:, b, h, g, :], xscales[:, b, h, g, :], g)
             if cg == 2:
                 for jp in range(2):
                     accv = psum.tile([P, 2, 2 * P], F32, tag="acc", name="accv", bufs=BANKS)
                     accs[(n, 2 + jp)] = accv
                     for jj in range(2):
-                        toks = slice((2 * jp + jj) * P, (2 * jp + jj + 1) * P)
+                        toks = slice(jj * P, (jj + 1) * P)
                         for g in range(2):
-                            mx(accv[:, jj, :], xcodes[:, b, g, toks], xscales[:, b, g, toks],
+                            mx(accv[:, jj, :], xcodes[:, b, jp, g, toks], xscales[:, b, jp, g, toks],
                                wvcodes[:, g, :], wvscales[:, g, :], g)
 
         def pool_units(n):
@@ -285,7 +294,7 @@ def tile_flashqwen2attention_pa_kernel(
                     vs = work.tile([P, 2, 2 * P], F32, tag="vs", name="vs", bufs=3)
                     nc.vector.tensor_tensor(
                         out=vs[:], in0=accs[(n, 2 + jp)][:],
-                        in1=bv[:].unsqueeze(1).to_broadcast([P, 2, 2 * P]), op=ALU.add,
+                        in1=bvraw[:].unsqueeze(1).to_broadcast([P, 2, 2 * P]), op=ALU.add,
                     )
                     r0 = b * S + jp * 2 * P
                     nc.sync.dma_start(out=v_out[r0:r0 + 2 * P, :].rearrange("(j p) c -> p j c", p=P), in_=vs[:])
@@ -322,8 +331,6 @@ def tile_flashqwen2attention_pa_kernel(
                 )
 
         bcol = keep.tile([P, NCT], F32, name="bcol")
-        bv = keep.tile([P, 2 * P], F32, name="bv")
-        brow32 = keep.tile([P, P], F32, name="brow32")
         x_widen(0, 0)
         x_widen(0, 1)
         w_turn(8, "acc")
@@ -332,29 +339,26 @@ def tile_flashqwen2attention_pa_kernel(
         x_turn(0, 0, "ob")
         x_unload(0, 0)
         w_unload(9)
-        nc.vector.tensor_copy(out=brow32[:], in_=brow[:])
         x_widen(0, 2)
         x_widen(0, 3)
         x_turn(0, 1, "ob")
         x_unload(0, 1)
-        bt = psum.tile([P, P], F32, tag="ob", name="bt", bufs=BANKS)
-        nc.tensor.transpose(out=bt[:], in_=brow32[:], identity=ident[:])
+        bt = psum.tile([P, P], BF16, tag="ob", name="bt", bufs=BANKS)
+        nc.tensor.transpose(out=bt[:], in_=brow[:], identity=ident_bf[:])
         w_turn(10, "acc")
         x_turn(0, 2, "ob")
         x_unload(0, 2)
         w_turn(11, "acc")
         x_turn(0, 3, "ob")
         x_unload(0, 3)
+        nc.scalar.copy(out=bcol[:], in_=bt[:, 0:NCT])
         w_quant(8)
         w_quant(9)
         x_quant(0, 0)
-        nc.vector.tensor_copy(out=bcol[:], in_=bt[:, 0:NCT])
-        nc.vector.tensor_copy(out=bv[:], in_=bvraw[:])
         x_quant(0, 2)
         w_unload(10)
         w_unload(11)
         w_quant(10)
-        w_quant(11)
 
         for n in range(STEPS):
             b, cg = STEP_LIST[n]
@@ -366,7 +370,8 @@ def tile_flashqwen2attention_pa_kernel(
             multiply(n)
             rotate(n)
             for j in nxt:
-                x_order(b + 1, j)
+                if b + 1 > 1:
+                    x_order(b + 1, j)
             jobs = [("x", j) for j in nxt]
             if n < 2:
                 cg_next = STEP_LIST[n + 1][1]

@@ -266,7 +266,7 @@ def tile_flashqwen2attention_pa_kernel(
 
         def pool_units(n):
             b, cg = STEP_LIST[n]
-            return (0, 1) if (b == 0 and cg < 2) else (0,)
+            return (0,)
 
         def rotate(n):
             b, cg = STEP_LIST[n]

@@ -92,15 +92,10 @@ def tile_flashqwen2attention_pa_kernel(
         ident = keep.tile([P, P], F32, name="ident")
         make_identity(nc, ident[:])
         perm = keep.tile([P, P], F32, name="perm")
-        nc.gpsimd.memset(perm[:], 0.0)
-        for base in (64, -64):
-            nc.gpsimd.affine_select(
-                out=perm[:], in_=perm[:], compare_op=ALU.not_equal, fill=1.0,
-                base=base, pattern=[[-1, P]], channel_multiplier=1,
-            )
-
+        nc.scalar.copy(out=perm[:, 0:64], in_=ident[:, 64:P])
+        nc.scalar.copy(out=perm[:, 64:P], in_=ident[:, 0:64])
         ident_bf = keep.tile([P, P], BF16, name="ident_bf")
-        make_identity(nc, ident_bf[:])
+        nc.scalar.copy(out=ident_bf[:], in_=ident[:])
 
         bits_i = keep.tile([P, 7], I32, name="bits_i")
         nc.vector.tensor_tensor(out=bits_i[:], in0=chan[:], in1=shift[:], op=ALU.logical_shift_right)
@@ -124,7 +119,7 @@ def tile_flashqwen2attention_pa_kernel(
         nc.vector.tensor_tensor(out=freq[:], in0=fac1[:], in1=fac3[:, 2:3], op=ALU.mult)
         sin_scale = keep.tile([P, 1], F32, name="sin_scale")
         nc.vector.tensor_scalar(
-            out=sin_scale[:], in0=bits[:, 6:7], scalar1=2.0 * TWO_PI, scalar2=-TWO_PI,
+            out=sin_scale[:], in0=bits[:, 6:7], scalar1=-2.0 * TWO_PI, scalar2=TWO_PI,
             op0=ALU.mult, op1=ALU.add,
         )
 
@@ -134,15 +129,13 @@ def tile_flashqwen2attention_pa_kernel(
         nc.vector.scalar_tensor_tensor(
             out=frac[:], in0=pos[:], scalar=freq[:, 0:1], in1=whole[:], op0=ALU.mult, op1=ALU.subtract
         )
-        negfrac = keep.tile([P, S], F32, name="negfrac")
-        nc.vector.scalar_tensor_tensor(
-            out=negfrac[:], in0=frac[:], scalar=0.5, in1=frac[:], op0=ALU.is_gt, op1=ALU.subtract
-        )
         absfrac = keep.tile([P, S], F32, name="absfrac")
-        nc.scalar.activation(out=absfrac[:], in_=negfrac[:], func=ACT.Abs)
         table = keep.tile([P, 2, S], F32, name="table")
-        nc.scalar.activation(out=table[:, 0, :], in_=absfrac[:], func=ACT.Sin, bias=0.5 * math.pi, scale=-TWO_PI)
-        nc.scalar.activation(out=table[:, 1, :], in_=negfrac[:], func=ACT.Sin, scale=sin_scale[:, 0:1])
+
+        def make_tables():
+            nc.scalar.activation(out=absfrac[:], in_=frac[:], func=ACT.Abs)
+            nc.scalar.activation(out=table[:, 0, :], in_=absfrac[:], func=ACT.Sin, bias=0.5 * math.pi, scale=-TWO_PI)
+            nc.scalar.activation(out=table[:, 1, :], in_=frac[:], func=ACT.Sin, scale=sin_scale[:, 0:1])
 
         xcodes = keep.tile([P, NB, 2, 2, S // 2], U32, name="xcodes", align_bytes=64)
         xscales = keep.tile([P, NB, 2, 2, S // 2], U8, name="xscales", align_bytes=64)
@@ -346,18 +339,19 @@ def tile_flashqwen2attention_pa_kernel(
         bt = psum.tile([P, P], BF16, tag="ob", name="bt", bufs=BANKS)
         nc.tensor.transpose(out=bt[:], in_=brow[:], identity=ident_bf[:])
         w_turn(10, "acc")
+        w_unload(10)
         x_turn(0, 2, "ob")
         x_unload(0, 2)
         w_turn(11, "acc")
+        w_unload(11)
         x_turn(0, 3, "ob")
         x_unload(0, 3)
         nc.scalar.copy(out=bcol[:], in_=bt[:, 0:NCT])
+        make_tables()
         w_quant(8)
         w_quant(9)
         x_quant(0, 0)
         x_quant(0, 2)
-        w_unload(10)
-        w_unload(11)
         w_quant(10)
 
         for n in range(STEPS):

@@ -292,36 +292,53 @@ def tile_flashqwen2attention_pa_kernel(
                     r0 = b * S + jp * 2 * P
                     nc.sync.dma_start(out=v_out[r0:r0 + 2 * P, :].rearrange("(j p) c -> p j c", p=P), in_=vs[:])
 
-        def turn_back(out, tu, toks):
-            nc.tensor.matmul(out=out, lhsT=tu[:, 0, toks], rhs=ident[:], is_transpose=True, start=True, stop=False)
-            nc.tensor.matmul(out=out, lhsT=tu[:, 1, toks], rhs=perm[:], is_transpose=True, start=False, stop=True)
-
         def blocks_of(n):
             return 4 if STEP_LIST[n][1] < 2 else 2
 
-        def finish_block(n, blk):
+        def store_block(n, blk, ob):
             b, cg = STEP_LIST[n]
             ys = work.tile([P, S], F32, tag="ys", name="ys", bufs=8)
+            nc.scalar.copy(out=ys[:], in_=ob[:])
             if cg < 2:
-                ob = psum.tile([P, S], F32, tag="ob", name="ob", bufs=BANKS)
-                toks = slice(blk * P, (blk + 1) * P)
-                for c4 in range(4):
-                    turn_back(ob[:, c4 * P:(c4 + 1) * P], tus[(n, c4)], toks)
-                nc.scalar.copy(out=ys[:], in_=ob[:])
                 r0 = b * S + blk * P
                 nc.sync.dma_start(out=q_out[r0:r0 + P, cg * S:(cg + 1) * S], in_=ys[:])
             else:
-                obk = psum.tile([P, 2, 2 * P], F32, tag="ob", name="obk", bufs=BANKS)
-                for jj in range(2):
-                    toks = slice((2 * blk + jj) * P, (2 * blk + jj + 1) * P)
-                    for c4 in range(2):
-                        turn_back(obk[:, jj, c4 * P:(c4 + 1) * P], tus[(n, c4)], toks)
-                nc.scalar.copy(out=ys[:], in_=obk[:].rearrange("p j c -> p (j c)"))
                 r0 = b * S + blk * 2 * P
                 nc.sync.dma_start(
                     out=k_out[r0:r0 + 2 * P, :].rearrange("(j p) c -> p j c", p=P),
                     in_=ys[:].rearrange("p (j c) -> p j c", j=2),
                 )
+
+        def block_transposes(n, blk):
+            if STEP_LIST[n][1] < 2:
+                groups = [(c4 * P, c4, slice(blk * P, (blk + 1) * P)) for c4 in range(4)]
+            else:
+                groups = [((2 * jj + c4) * P, c4, slice((2 * blk + jj) * P, (2 * blk + jj + 1) * P))
+                          for jj in range(2) for c4 in range(2)]
+            return [(blk, col, c4, toks, part) for (col, c4, toks) in groups for part in range(2)]
+
+        def finish_blocks(n):
+            nblk = blocks_of(n)
+            even = [op for blk in range(0, nblk, 2) for op in block_transposes(n, blk)]
+            odd = [op for blk in range(1, nblk, 2) for op in block_transposes(n, blk)]
+            order = even[0:4]
+            for i in range(len(odd)):
+                order.extend(even[4 + i:5 + i])
+                order.append(odd[i])
+            banks = {}
+            done = {}
+            for (blk, col, c4, toks, part) in order:
+                if blk not in banks:
+                    ob = psum.tile([P, S], F32, tag="ob", name="ob", bufs=BANKS)
+                    banks[blk] = ob
+                    done[blk] = 0
+                nc.tensor.matmul(
+                    out=banks[blk][:, col:col + P], lhsT=tus[(n, c4)][:, part, toks],
+                    rhs=(ident[:] if part == 0 else perm[:]), is_transpose=True, start=(part == 0), stop=(part == 1),
+                )
+                done[blk] = done[blk] + 1
+                if done[blk] == 8:
+                    store_block(n, blk, banks[blk])
 
         bcol = keep.tile([P, NCT], F32, name="bcol")
         x_widen(0, 0)
@@ -370,20 +387,16 @@ def tile_flashqwen2attention_pa_kernel(
             if n < 2:
                 cg_next = STEP_LIST[n + 1][1]
                 jobs = [("w", ct) for ct in range(4 * cg_next, 4 * cg_next + 4)] + jobs
-            nblk = blocks_of(n - 1) if n > 0 else 0
-            for i in range(max(nblk, len(jobs))):
-                if i < len(jobs):
-                    kind, idx = jobs[i]
-                    if kind == "w":
-                        w_turn(idx, "ob")
-                        w_unload(idx)
-                        w_quant(idx)
-                    else:
-                        x_turn(b + 1, idx, "ob")
-                        x_unload(b + 1, idx)
-                        if idx % 2 == 1:
-                            x_quant(b + 1, idx - 1)
-                if i < nblk:
-                    finish_block(n - 1, i)
-        for blk in range(blocks_of(STEPS - 1)):
-            finish_block(STEPS - 1, blk)
+            for (kind, idx) in jobs:
+                if kind == "w":
+                    w_turn(idx, "ob")
+                    w_unload(idx)
+                    w_quant(idx)
+                else:
+                    x_turn(b + 1, idx, "ob")
+                    x_unload(b + 1, idx)
+                    if idx % 2 == 1:
+                        x_quant(b + 1, idx - 1)
+            if n > 0:
+                finish_blocks(n - 1)
+        finish_blocks(STEPS - 1)

@@ -137,13 +137,13 @@ def tile_flashqwen2attention_pa_kernel(
             nc.scalar.activation(out=table[:, 0, :], in_=absfrac[:], func=ACT.Sin, bias=0.5 * math.pi, scale=-TWO_PI)
             nc.scalar.activation(out=table[:, 1, :], in_=frac[:], func=ACT.Sin, scale=sin_scale[:, 0:1])
 
-        xcodes = keep.tile([P, NB, 2, 2, S // 2], U32, name="xcodes", align_bytes=64)
-        xscales = keep.tile([P, NB, 2, 2, S // 2], U8, name="xscales", align_bytes=64)
-        wcodes = keep.tile([P, NCT, 2, P], U32, name="wcodes", align_bytes=64)
-        wscales = keep.tile([P, NCT, 2, P], U8, name="wscales", align_bytes=64)
+        xcodes = keep.tile([P, NB, 2, 2, S // 2], U32, name="xcodes", align_bytes=256)
+        xscales = keep.tile([P, NB, 2, 2, S // 2], U8, name="xscales", align_bytes=256)
+        wcodes = keep.tile([P, NCT, 2, P], U32, name="wcodes", align_bytes=256)
+        wscales = keep.tile([P, NCT, 2, P], U8, name="wscales", align_bytes=256)
 
-        wvcodes = keep.tile([P, 2, 2 * P], U32, name="wvcodes", align_bytes=64)
-        wvscales = keep.tile([P, 2, 2 * P], U8, name="wvscales", align_bytes=64)
+        wvcodes = keep.tile([P, 2, 2 * P], U32, name="wvcodes", align_bytes=256)
+        wvscales = keep.tile([P, 2, 2 * P], U8, name="wvscales", align_bytes=256)
 
         turned = {}
 

from contextlib import ExitStack
import math

import concourse.mybir as mybir
from concourse.masks import make_identity

F32 = mybir.dt.float32
BF16 = mybir.dt.bfloat16
I32 = mybir.dt.int32
U8 = mybir.dt.uint8
U32 = mybir.dt.uint32
FP8 = mybir.dt.float8_e4m3fn
FP8X4 = mybir.dt.float8_e4m3fn_x4
ALU = mybir.AluOpType
ACT = mybir.ActivationFunctionType

P = 128
NB = 4
S = 512
D = 1024
NCT = 12
NROPE = 10
STEP_LIST = [(0, 2), (0, 0), (0, 1)] + [(b, cg) for b in range(1, NB) for cg in range(3)]
STEPS = len(STEP_LIST)
BANKS = 4
FLOPS = 2 * 2048 * 1024 * 1536
TWO_PI = 2.0 * math.pi


def tile_flashqwen2attention_pa_kernel(
    tc, hidden_states_bytes, hidden_states_scale, wqkv, bqkv, out_0, out_1, out_2
):
    nc = tc.nc
    q_out = out_0.rearrange("b s h d -> (b s) (h d)")
    k_out = out_1.rearrange("b s h d -> (b s) (h d)")
    v_out = out_2.rearrange("b s h d -> (b s) (h d)")
    x_rows = hidden_states_bytes.rearrange("(b j p) k -> b p j k", j=4, p=P)

    with ExitStack() as ctx:
        keep = ctx.enter_context(tc.tile_pool(name="keep", bufs=1))
        work = ctx.enter_context(tc.tile_pool(name="work", bufs=2))
        psum = ctx.enter_context(tc.psum_pool(name="psum", bufs=1))
        ctx.enter_context(tc.manual_schedule())

        brow = keep.tile([P, P], BF16, name="brow")
        nc.gpsimd.memset(brow[:], 0.0)
        sc = keep.tile([P, D], F32, name="sc")
        nc.scalar.dma_start(
            out=sc[:], in_=hidden_states_scale.rearrange("o k -> (o k)").partition_broadcast(P)
        )
        nc.scalar.dma_start(out=brow[0:NCT, :], in_=bqkv.rearrange("(t p) -> t p", p=P))
        bvraw = keep.tile([P, 2 * P], BF16, name="bvraw")
        nc.scalar.dma_start(out=bvraw[:], in_=bqkv[NROPE * P:NCT * P].partition_broadcast(P))

        xbytes = []
        for b in range(NB):
            xbytes_b = keep.tile([P, 4, D], U8, name="xbytes%d" % b)
            xbytes.append(xbytes_b)
        wraw = []
        for ct in range(NCT):
            wraw_ct = keep.tile([P, D], BF16, name="wraw%d" % ct)
            wraw.append(wraw_ct)

        def load_x(b):
            nc.sync.dma_start(out=xbytes[b][:], in_=x_rows[b])

        def load_w(ct):
            nc.sync.dma_start(out=wraw[ct][:], in_=wqkv[ct * P:(ct + 1) * P, :])

        for j in range(4):
            nc.sync.dma_start(out=xbytes[0][:, j, :], in_=x_rows[0][:, j, :])
            load_w(8 + j)
        for ct in range(0, 4):
            load_w(ct)
        load_x(1)
        for ct in range(4, 8):
            load_w(ct)
        load_x(2)
        load_x(3)

        warm = keep.tile([P, 1], F32, name="warm")
        nc.gpsimd.memset(warm[:], 0.0)
        warm2 = keep.tile([P, 1], F32, name="warm2")
        nc.scalar.activation(out=warm2[:], in_=warm[:], func=ACT.Sin)

        chan = keep.tile([P, 7], I32, name="chan")
        nc.gpsimd.iota(chan[:], pattern=[[0, 7]], base=0, channel_multiplier=1)
        shift = keep.tile([P, 7], I32, name="shift")
        nc.gpsimd.iota(shift[:], pattern=[[1, 7]], base=0, channel_multiplier=0)
        pos = keep.tile([P, S], I32, name="pos")
        nc.gpsimd.iota(pos[:], pattern=[[1, S]], base=0, channel_multiplier=0)
        ident = keep.tile([P, P], F32, name="ident")
        make_identity(nc, ident[:])
        perm = keep.tile([P, P], F32, name="perm")
        nc.scalar.copy(out=perm[:, 0:64], in_=ident[:, 64:P])
        nc.scalar.copy(out=perm[:, 64:P], in_=ident[:, 0:64])
        ident_bf = keep.tile([P, P], BF16, name="ident_bf")
        nc.scalar.copy(out=ident_bf[:], in_=ident[:])

        bits_i = keep.tile([P, 7], I32, name="bits_i")
        nc.vector.tensor_tensor(out=bits_i[:], in0=chan[:], in1=shift[:], op=ALU.logical_shift_right)
        bits_j = keep.tile([P, 7], I32, name="bits_j")
        nc.vector.tensor_scalar(out=bits_j[:], in0=bits_i[:], scalar1=1, scalar2=None, op0=ALU.bitwise_and)
        bits = keep.tile([P, 7], F32, name="bits")
        nc.vector.tensor_copy(out=bits[:], in_=bits_j[:])
        fac = keep.tile([P, 6], F32, name="fac")
        for bit in range(6):
            ratio = 10000.0 ** (-(2.0 ** bit) / 64.0)
            lead = 1.0 / TWO_PI if bit == 0 else 1.0
            nc.vector.tensor_scalar(
                out=fac[:, bit:bit + 1], in0=bits[:, bit:bit + 1],
                scalar1=(ratio - 1.0) * lead, scalar2=lead, op0=ALU.mult, op1=ALU.add,
            )
        fac3 = keep.tile([P, 3], F32, name="fac3")
        nc.vector.tensor_tensor(out=fac3[:], in0=fac[:, 0:3], in1=fac[:, 3:6], op=ALU.mult)
        fac1 = keep.tile([P, 1], F32, name="fac1")
        nc.vector.tensor_tensor(out=fac1[:], in0=fac3[:, 0:1], in1=fac3[:, 1:2], op=ALU.mult)
        freq = keep.tile([P, 1], F32, name="freq")
        nc.vector.tensor_tensor(out=freq[:], in0=fac1[:], in1=fac3[:, 2:3], op=ALU.mult)
        sin_scale = keep.tile([P, 1], F32, name="sin_scale")
        nc.vector.tensor_scalar(
            out=sin_scale[:], in0=bits[:, 6:7], scalar1=-2.0 * TWO_PI, scalar2=TWO_PI,
            op0=ALU.mult, op1=ALU.add,
        )

        whole = keep.tile([P, S], I32, name="whole")
        nc.vector.tensor_scalar(out=whole[:], in0=pos[:], scalar1=freq[:, 0:1], scalar2=None, op0=ALU.mult)
        frac = keep.tile([P, S], F32, name="frac")
        nc.vector.scalar_tensor_tensor(
            out=frac[:], in0=pos[:], scalar=freq[:, 0:1], in1=whole[:], op0=ALU.mult, op1=ALU.subtract
        )
        absfrac = keep.tile([P, S], F32, name="absfrac")
        table = keep.tile([P, 2, S], F32, name="table")

        def make_tables():
            nc.scalar.activation(out=absfrac[:], in_=frac[:], func=ACT.Abs)
            nc.scalar.activation(out=table[:, 0, :], in_=absfrac[:], func=ACT.Sin, bias=0.5 * math.pi, scale=-TWO_PI)
            nc.scalar.activation(out=table[:, 1, :], in_=frac[:], func=ACT.Sin, scale=sin_scale[:, 0:1])

        xcodes = keep.tile([P, NB, 2, 2, S // 2], U32, name="xcodes", align_bytes=256)
        xscales = keep.tile([P, NB, 2, 2, S // 2], U8, name="xscales", align_bytes=256)
        wcodes = keep.tile([P, NCT, 2, P], U32, name="wcodes", align_bytes=256)
        wscales = keep.tile([P, NCT, 2, P], U8, name="wscales", align_bytes=256)

        wvcodes = keep.tile([P, 2, 2 * P], U32, name="wvcodes", align_bytes=256)
        wvscales = keep.tile([P, 2, 2 * P], U8, name="wvscales", align_bytes=256)

        turned = {}

        def every_second_word(rows_bf16):
            words = rows_bf16.bitcast(F32)
            return [[words[:, 256 * g + u:256 * (g + 1):2] for u in range(2)] for g in range(2)]

        def turn(key, quarters, tag):
            bank = psum.tile([P, 2, 2, P], F32, tag=tag, name=tag, bufs=BANKS)
            turned[key] = bank
            for g in range(2):
                for u in range(2):
                    nc.tensor.transpose(out=bank[:, g, u, :], in_=quarters[g][u], identity=ident[:])

        def unload(key, dst_words):
            nc.scalar.copy(out=dst_words, in_=turned[key][:].rearrange("p g u r -> p g r u"))

        wg = {}

        def w_turn(ct, tag):
            turn(("w", ct), every_second_word(wraw[ct][:]), tag)

        wgv = keep.tile([P, 2, 2 * P, 4], BF16, name="wgv", align_bytes=64)

        def w_unload(ct):
            if ct >= NROPE:
                cols = slice((ct - NROPE) * P, (ct - NROPE + 1) * P)
                unload(("w", ct), wgv[:].bitcast(F32)[:, :, cols, :])
                return
            wg_ct = work.tile([P, 2, P, 4], BF16, tag="wg", name="wg", bufs=4, align_bytes=64)
            wg[ct] = wg_ct
            unload(("w", ct), wg_ct[:].bitcast(F32))

        def w_quant(ct):
            if ct >= NROPE:
                nc.vector.quantize_mx(
                    out=wvcodes[:].rearrange("p g c -> p (g c)").bitcast(FP8X4),
                    scales=wvscales[:].rearrange("p g c -> p (g c)"),
                    in_=wgv[:].rearrange("p g c t -> p (g c t)"),
                )
                return
            nc.vector.quantize_mx(
                out=wcodes[:, ct].rearrange("p g m -> p (g m)").bitcast(FP8X4),
                scales=wscales[:, ct].rearrange("p g m -> p (g m)"),
                in_=wg[ct][:].rearrange("p g m t -> p (g m t)"),
            )

        xw = {}
        xg = {}

        def x_widen(b, j):
            xw_t = work.tile([P, D], BF16, tag="xw", name="xw", bufs=4)
            xw[(b, j)] = xw_t
            nc.vector.tensor_tensor(out=xw_t[:], in0=xbytes[b][:, j, :].bitcast(FP8), in1=sc[:], op=ALU.mult)

        xp = {}

        def x_order(b, j):
            xp_t = work.tile([P, 2, 2, P], F32, tag="xp", name="xp", bufs=3)
            xp[(b, j)] = xp_t
            nc.scalar.copy(out=xp_t[:], in_=xw[(b, j)][:].bitcast(F32).rearrange("p (g w u) -> p g u w", g=2, u=2))

        def x_turn(b, j, tag):
            if b <= 1:
                quarters = every_second_word(xw[(b, j)][:])
            else:
                quarters = [[xp[(b, j)][:, g, u, :] for u in range(2)] for g in range(2)]
            turn(("x", b, j), quarters, tag)

        def x_unload(b, j):
            if j == 0:
                xg_b = work.tile([P, 2, 2, S // 2, 4], BF16, tag="xg", name="xg", bufs=2, align_bytes=64)
                xg[b] = xg_b
            unload(("x", b, j), xg[b][:, j // 2].bitcast(F32)[:, :, (j % 2) * P:(j % 2 + 1) * P, :])

        def x_quant(b, j0):
            h = j0 // 2
            nc.vector.quantize_mx(
                out=xcodes[:, b, h].rearrange("p g r -> p (g r)").bitcast(FP8X4),
                scales=xscales[:, b, h].rearrange("p g r -> p (g r)"),
                in_=xg[b][:, h].rearrange("p g r t -> p (g r t)"),
            )

        accs = {}
        tus = {}

        def mx(out, lhs, lhs_s, rhs, rhs_s, g):
            nc.tensor.matmul_mx(out=out, lhsT=lhs.bitcast(FP8X4), lhsT_scale=lhs_s,
                                rhs=rhs.bitcast(FP8X4), rhs_scale=rhs_s, start=(g == 0), stop=(g == 1))

        def rope_units(cg):
            return range(4) if cg < 2 else range(2)

        def multiply(n):
            b, cg = STEP_LIST[n]
            for c4 in rope_units(cg):
                ct = 4 * cg + c4
                acc = psum.tile([P, S], F32, tag="acc", name="acc", bufs=BANKS)
                accs[(n, c4)] = acc
                for h in range(2):
                    for g in range(2):
                        mx(acc[:, h * (S // 2):(h + 1) * (S // 2)], wcodes[:, ct, g, :], wscales[:, ct, g, :],
                           xcodes[:, b, h, g, :], xscales[:, b, h, g, :], g)
            if cg == 2:
                for jp in range(2):
                    accv = psum.tile([P, 2, 2 * P], F32, tag="acc", name="accv", bufs=BANKS)
                    accs[(n, 2 + jp)] = accv
                    for jj in range(2):
                        toks = slice(jj * P, (jj + 1) * P)
                        for g in range(2):
                            mx(accv[:, jj, :], xcodes[:, b, jp, g, toks], xscales[:, b, jp, g, toks],
                               wvcodes[:, g, :], wvscales[:, g, :], g)

        def pool_units(n):
            b, cg = STEP_LIST[n]
            return (0,)

        def rotate(n):
            b, cg = STEP_LIST[n]
            on_pool = pool_units(n)
            for c4 in rope_units(cg):
                ct = 4 * cg + c4
                acc = accs[(n, c4)]
                tu = work.tile([P, 2, S], F32, tag="tu", name="tu", bufs=8)
                tus[(n, c4)] = tu
                if c4 in on_pool:
                    xs = work.tile([P, S], F32, tag="xs", name="xs", bufs=3)
                    nc.scalar.activation(
                        out=xs[:], in_=acc[:], func=ACT.Identity, bias=bcol[:, ct:ct + 1], scale=1.0
                    )
                    nc.gpsimd.tensor_tensor(
                        out=tu[:], in0=xs[:].unsqueeze(1).to_broadcast([P, 2, S]), in1=table[:], op=ALU.mult
                    )
                else:
                    nc.vector.scalar_tensor_tensor(
                        out=tu[:], in0=acc[:].unsqueeze(1).to_broadcast([P, 2, S]),
                        scalar=bcol[:, ct:ct + 1], in1=table[:], op0=ALU.add, op1=ALU.mult,
                    )
            if cg == 2:
                for jp in range(2):
                    vs = work.tile([P, 2, 2 * P], F32, tag="vs", name="vs", bufs=3)
                    nc.vector.tensor_tensor(
                        out=vs[:], in0=accs[(n, 2 + jp)][:],
                        in1=bvraw[:].unsqueeze(1).to_broadcast([P, 2, 2 * P]), op=ALU.add,
                    )
                    r0 = b * S + jp * 2 * P
                    nc.sync.dma_start(out=v_out[r0:r0 + 2 * P, :].rearrange("(j p) c -> p j c", p=P), in_=vs[:])

        def blocks_of(n):
            return 4 if STEP_LIST[n][1] < 2 else 2

        def store_block(n, blk, ob):
            b, cg = STEP_LIST[n]
            ys = work.tile([P, S], F32, tag="ys", name="ys", bufs=8)
            nc.scalar.copy(out=ys[:], in_=ob[:])
            if cg < 2:
                r0 = b * S + blk * P
                nc.sync.dma_start(out=q_out[r0:r0 + P, cg * S:(cg + 1) * S], in_=ys[:])
            else:
                r0 = b * S + blk * 2 * P
                nc.sync.dma_start(
                    out=k_out[r0:r0 + 2 * P, :].rearrange("(j p) c -> p j c", p=P),
                    in_=ys[:].rearrange("p (j c) -> p j c", j=2),
                )

        def block_transposes(n, blk):
            if STEP_LIST[n][1] < 2:
                groups = [(c4 * P, c4, slice(blk * P, (blk + 1) * P)) for c4 in range(4)]
            else:
                groups = [((2 * jj + c4) * P, c4, slice((2 * blk + jj) * P, (2 * blk + jj + 1) * P))
                          for jj in range(2) for c4 in range(2)]
            return [(blk, col, c4, toks, part) for (col, c4, toks) in groups for part in range(2)]

        def finish_blocks(n):
            nblk = blocks_of(n)
            even = [op for blk in range(0, nblk, 2) for op in block_transposes(n, blk)]
            odd = [op for blk in range(1, nblk, 2) for op in block_transposes(n, blk)]
            order = even[0:4]
            for i in range(len(odd)):
                order.extend(even[4 + i:5 + i])
                order.append(odd[i])
            banks = {}
            done = {}
            for (blk, col, c4, toks, part) in order:
                if blk not in banks:
                    ob = psum.tile([P, S], F32, tag="ob", name="ob", bufs=BANKS)
                    banks[blk] = ob
                    done[blk] = 0
                nc.tensor.matmul(
                    out=banks[blk][:, col:col + P], lhsT=tus[(n, c4)][:, part, toks],
                    rhs=(ident[:] if part == 0 else perm[:]), is_transpose=True, start=(part == 0), stop=(part == 1),
                )
                done[blk] = done[blk] + 1
                if done[blk] == 8:
                    store_block(n, blk, banks[blk])

        bcol = keep.tile([P, NCT], F32, name="bcol")
        x_widen(0, 0)
        x_widen(0, 1)
        w_turn(8, "acc")
        w_unload(8)
        w_turn(9, "acc")
        x_turn(0, 0, "ob")
        x_unload(0, 0)
        w_unload(9)
        x_widen(0, 2)
        x_widen(0, 3)
        x_turn(0, 1, "ob")
        x_unload(0, 1)
        bt = psum.tile([P, P], BF16, tag="ob", name="bt", bufs=BANKS)
        nc.tensor.transpose(out=bt[:], in_=brow[:], identity=ident_bf[:])
        w_turn(10, "acc")
        w_unload(10)
        x_turn(0, 2, "ob")
        x_unload(0, 2)
        w_turn(11, "acc")
        w_unload(11)
        x_turn(0, 3, "ob")
        x_unload(0, 3)
        nc.scalar.copy(out=bcol[:], in_=bt[:, 0:NCT])
        make_tables()
        w_quant(8)
        w_quant(9)
        x_quant(0, 0)
        x_quant(0, 2)
        w_quant(10)

        for n in range(STEPS):
            b, cg = STEP_LIST[n]
            nxt = []
            if b + 1 < NB:
                nxt = [(0,), (1,), (2, 3)][n % 3]
            for j in nxt:
                x_widen(b + 1, j)
            multiply(n)
            rotate(n)
            for j in nxt:
                if b + 1 > 1:
                    x_order(b + 1, j)
            jobs = [("x", j) for j in nxt]
            if n < 2:
                cg_next = STEP_LIST[n + 1][1]
                jobs = [("w", ct) for ct in range(4 * cg_next, 4 * cg_next + 4)] + jobs
            for (kind, idx) in jobs:
                if kind == "w":
                    w_turn(idx, "ob")
                    w_unload(idx)
                    w_quant(idx)
                else:
                    x_turn(b + 1, idx, "ob")
                    x_unload(b + 1, idx)
                    if idx % 2 == 1:
                        x_quant(b + 1, idx - 1)
            if n > 0:
                finish_blocks(n - 1)
        finish_blocks(STEPS - 1)
